import numpy as np
import ml_dtypes


def mxq(x, axis, fmt="e4m3"):
    dtype, down = {"e4m3": (ml_dtypes.float8_e4m3fn, 7), "e5m2": (ml_dtypes.float8_e5m2, 14)}[fmt]
    v = np.moveaxis(np.asarray(x, np.float32).astype(ml_dtypes.bfloat16).astype(np.float64), axis, -1)
    blocks = v.reshape(v.shape[:-1] + (-1, 32))
    amax = np.abs(blocks).max(-1, keepdims=True)
    byte = np.maximum(np.where(amax > 0, np.frexp(amax)[1] - 1 + 127, 0) - down, 1)
    scale = np.exp2(byte - 127.0)
    codes = (blocks / scale).astype(np.float32).astype(dtype).astype(np.float64)
    return np.moveaxis((codes * scale).reshape(v.shape), -1, axis)


WIDE = False


def mx_kscale(k):
    if not WIDE:
        return np.ones(k)
    levels = np.array([10, -10, 5, -5, 0])
    a = np.random.permutation(np.resize(levels, k // 512 * 4)).reshape(k // 512, 4)
    idx = np.arange(k)
    return np.exp2(a[idx // 512, idx % 128 // 32])


BF16 = ml_dtypes.bfloat16


def bf(x):
    return np.asarray(x, np.float32).astype(BF16)


def f64(x):
    return np.asarray(x).astype(np.float64)


B, T, N, D, H, F = 1, 512, 2, 1024, 8, 1024
S = B * N
EPS = 1e-5


def layernorm(v, g, b):
    mu = v.mean(-1, keepdims=True)
    var = np.square(v - mu).mean(-1, keepdims=True)
    return (v - mu) / np.sqrt(var + EPS) * g + b


def setup_inputs():
    s = mx_kscale(D)
    t = mx_kscale(D)
    return {"ax_cat": bf(np.random.standard_normal((S, T, D)) * 4.0 * s),
            "features": bf(np.random.standard_normal((B, T, N, D))),
            "wout_w": bf(np.random.standard_normal((D, D)) * 0.5 / np.sqrt(D) / s),
            "ln_g": bf((1.0 + 0.1 * np.random.standard_normal(D)) * t),
            "ln_b": bf(0.1 * np.random.standard_normal(D) * t),
            "ff1_w": bf(np.random.standard_normal((F, D)) / np.sqrt(D) / t),
            "ff1_b": bf(0.1 * np.random.standard_normal(F))}


def reference(ax_cat, features, wout_w, ln_g, ln_b, ff1_w, ff1_b):
    x = f64(features).transpose(0, 2, 1, 3).reshape(S, T, D)
    y = mxq(f64(ax_cat), 2, "e4m3") @ mxq(f64(wout_w), 1, "e4m3").T
    m = layernorm(y + x, f64(ln_g), f64(ln_b))
    return np.maximum((mxq(m, 2, "e4m3") @ mxq(f64(ff1_w), 1, "e4m3").T) + f64(ff1_b), 0.0)

@@ -1,0 +1,348 @@
+from contextlib import ExitStack
+
+import concourse.mybir as mybir
+from concourse.masks import make_identity
+
+F32 = mybir.dt.float32
+BF16 = mybir.dt.bfloat16
+U32 = mybir.dt.uint32
+U8 = mybir.dt.uint8
+FP8X4 = mybir.dt.float8_e4m3fn_x4
+ACT = mybir.ActivationFunctionType
+ALU = mybir.AluOpType
+
+P = 128
+PACK = 4
+D = 1024
+PASSES = D // (P * PACK)
+BANK = 512
+HALVES = D // BANK
+ROW_BLOCKS = D // P
+SEQS = 2
+TIME_BLOCKS = 4
+TOKEN_BLOCKS = SEQS * TIME_BLOCKS
+EPS = 1e-5
+
+FLOPS = 2 * 2 * (SEQS * 512) * D * D
+
+
+def tile_temporalatt_pb_kernel(tc, ax_cat, features, wout_w, ln_g, ln_b, ff1_w, ff1_b, out):
+    nc = tc.nc
+
+    ax_view = ax_cat.rearrange("s (b p) k -> p b s k", p=P)
+    x_view = features.rearrange("o (b p) s d -> p (o b) s d", p=P)
+    out_view = out.rearrange("s (b p) f -> p b s f", p=P)
+    wout_view = wout_w.rearrange("(c p e) k -> p e c k", p=P, e=2)
+    ff1_view = ff1_w.rearrange("(j p) k -> p j k", p=P)
+
+    with ExitStack() as stack:
+        stack.enter_context(tc.manual_schedule())
+        keep = stack.enter_context(tc.tile_pool(name="keep", bufs=1))
+        stage = stack.enter_context(tc.tile_pool(name="stage", bufs=2))
+        stats = stack.enter_context(tc.tile_pool(name="stats", bufs=4))
+        results = stack.enter_context(tc.tile_pool(name="results", bufs=3))
+        psum_t = stack.enter_context(tc.psum_pool(name="psum_t", bufs=4))
+        psum_mm = stack.enter_context(tc.psum_pool(name="psum_mm", bufs=4))
+
+        ident = keep.tile([P, P], F32)
+        make_identity(nc, ident[:])
+        ones = keep.tile([P, P], BF16)
+        nc.gpsimd.memset(ones[:], 1.0)
+        bias_row = keep.tile([P, D], BF16)
+        nc.gpsimd.memset(bias_row[:], 0.0)
+        ln_rows = keep.tile([P, 2 * P], BF16)
+        nc.gpsimd.memset(ln_rows[:], 0.0)
+        eps_col = keep.tile([P, 1], F32)
+        nc.vector.memset(eps_col[:], EPS)
+        warm = keep.tile([P, 1], F32)
+        nc.scalar.activation(out=warm[:], in_=eps_col[:], func=ACT.Sqrt)
+
+        nc.scalar.dma_start(out=ln_rows[0:4, :], in_=ln_g.rearrange("(c w) -> c w", c=4))
+        nc.scalar.dma_start(out=ln_rows[4:8, :], in_=ln_b.rearrange("(c w) -> c w", c=4))
+        nc.scalar.dma_start(out=bias_row[0:1, :], in_=ff1_b.rearrange("(o f) -> o f", o=1))
+
+        wout_raw = keep.tile([P, 2, 4, D], BF16)
+        ax_raw = keep.tile([P, TIME_BLOCKS, SEQS, D], BF16)
+        x_raw = keep.tile([P, TIME_BLOCKS, SEQS, D], BF16)
+        ff1_raw = keep.tile([P, ROW_BLOCKS, D], BF16)
+
+        def load_ax(b):
+            nc.sync.dma_start(out=ax_raw[:, b], in_=ax_view[:, b])
+
+        def load_x(b):
+            nc.sync.dma_start(out=x_raw[:, b], in_=x_view[:, b])
+
+        def load_ff1(j):
+            nc.sync.dma_start(out=ff1_raw[:, j : j + 2], in_=ff1_view[:, j : j + 2])
+
+        load_ax(0)
+        for e in range(2):
+            for c in range(0, 4, 2):
+                nc.sync.dma_start(out=wout_raw[:, e, c : c + 2], in_=wout_view[:, e, c : c + 2])
+        load_x(0)
+        load_ax(1)
+        load_ax(2)
+        load_x(1)
+        load_ax(3)
+        load_ff1(0)
+        load_ff1(2)
+        load_x(2)
+        load_ff1(4)
+        load_ff1(6)
+        load_x(3)
+
+        w1_codes = keep.tile([P, HALVES, PASSES, BANK], U32, align_bytes=64)
+        w1_scales = keep.tile([P, HALVES, PASSES, BANK], U8, align_bytes=64)
+        w2_codes = keep.tile([P, HALVES, PASSES, BANK], U32, align_bytes=64)
+        w2_scales = keep.tile([P, HALVES, PASSES, BANK], U8, align_bytes=64)
+        a_codes = keep.tile([P, TOKEN_BLOCKS, PASSES, P], U32, align_bytes=64)
+        a_scales = keep.tile([P, TOKEN_BLOCKS, PASSES, P], U8, align_bytes=64)
+        m_codes = keep.tile([P, TOKEN_BLOCKS, PASSES, P], U32, align_bytes=64)
+        m_scales = keep.tile([P, TOKEN_BLOCKS, PASSES, P], U8, align_bytes=64)
+
+        def turn_rows(raw_rows):
+            words = raw_rows.bitcast(F32)
+            bank = psum_t.tile([P, 4, P], F32, tag="turned")
+            for c in range(4):
+                nc.tensor.transpose(bank[:, c, :], words[:, c * P : (c + 1) * P], ident[:])
+            return bank
+
+        def group_rows(copy, bank, grouped_rows):
+            copy(out=grouped_rows.bitcast(F32), in_=bank[:].rearrange("p (g u) r -> p g r u", u=2))
+
+        def quantise(grouped, codes, scales):
+            nc.vector.quantize_mx(
+                out=codes.rearrange("p g r -> p (g r)").bitcast(FP8X4),
+                scales=scales.rearrange("p g r -> p (g r)"),
+                in_=grouped.rearrange("p g r t -> p (g r t)"),
+            )
+
+        def matmul_group(lhs_codes, lhs_scales, rhs_codes, rhs_scales):
+            acc = psum_mm.tile([P, BANK], F32, tag="acc")
+            for g in range(PASSES):
+                nc.tensor.matmul_mx(
+                    out=acc[:],
+                    lhsT=lhs_codes[:, g, :].bitcast(FP8X4),
+                    lhsT_scale=lhs_scales[:, g, :],
+                    rhs=rhs_codes[:, g, :].bitcast(FP8X4),
+                    rhs_scale=rhs_scales[:, g, :],
+                    start=(g == 0),
+                    stop=(g == PASSES - 1),
+                )
+            return acc
+
+        def prepare_tokens(b, copies):
+            a_grouped = stage.tile([P, SEQS * PASSES, P, PACK], BF16, align_bytes=64, tag="a_grouped", bufs=3)
+            for s in range(SEQS):
+                bank = turn_rows(ax_raw[:, b, s, :])
+                group_rows(copies[s], bank, a_grouped[:, s * PASSES : (s + 1) * PASSES])
+            return a_grouped
+
+        def quantise_tokens(b, a_grouped):
+            first = SEQS * b
+            nc.vector.quantize_mx(
+                out=a_codes[:, first : first + SEQS].rearrange("p i g r -> p (i g r)").bitcast(FP8X4),
+                scales=a_scales[:, first : first + SEQS].rearrange("p i g r -> p (i g r)"),
+                in_=a_grouped[:].rearrange("p g r t -> p (g r t)"),
+            )
+
+        def prepare_weight_rows(raw_rows, copy, w_grouped, c):
+            group_rows(copy, turn_rows(raw_rows), w_grouped[:, :, c * P : (c + 1) * P, :])
+
+        def new_w_grouped():
+            w_grouped = stage.tile([P, PASSES, BANK, PACK], BF16, align_bytes=64, tag="w_grouped")
+            return w_grouped
+
+        y_banks = {}
+        r_tiles = {}
+        neg_means = {}
+        stds = {}
+        z_tiles = {}
+        zt_banks = {}
+        plane_tiles = {}
+        m_groupeds = {}
+        o_banks = {}
+        result_tiles = {}
+
+        def project(i):
+            y_banks[i] = [
+                matmul_group(a_codes[:, i], a_scales[:, i], w1_codes[:, e], w1_scales[:, e])
+                for e in range(HALVES)
+            ]
+
+        def add_residual(i):
+            b, s = divmod(i, SEQS)
+            r = stage.tile([P, D], F32, tag="r", bufs=4)
+            sums = stats.tile([P, HALVES], F32, tag="sums")
+            x_even_odd = x_raw[:, b, s, :].rearrange("p (q e) -> p e q", e=2)
+            for e in range(HALVES):
+                nc.vector.scalar_tensor_tensor(
+                    out=r[:, e * BANK : (e + 1) * BANK],
+                    in0=y_banks[i][e][:],
+                    scalar=1.0,
+                    in1=x_even_odd[:, e, :],
+                    op0=ALU.mult,
+                    op1=ALU.add,
+                    accum_out=sums[:, e : e + 1],
+                )
+            r_tiles[i] = r
+            return sums
+
+        def deviation(i, sums):
+            scaled = stats.tile([P, HALVES], F32, tag="scaled")
+            neg_mean = stats.tile([P, 1], F32, tag="neg_mean")
+            nc.scalar.activation(
+                out=scaled[:], in_=sums[:], func=ACT.Identity, scale=-1.0 / D, accum_out=neg_mean[:]
+            )
+            squares = stage.tile([P, D], BF16, tag="squares")
+            sum_sq = stats.tile([P, 1], F32, tag="sum_sq")
+            nc.scalar.activation(
+                out=squares[:], in_=r_tiles[i][:], func=ACT.Square, bias=neg_mean[:], accum_out=sum_sq[:]
+            )
+            std = stats.tile([P, 1], F32, tag="std")
+            nc.scalar.activation(out=std[:], in_=sum_sq[:], func=ACT.Sqrt, scale=1.0 / D, bias=eps_col[:])
+            neg_means[i] = neg_mean
+            stds[i] = std
+
+        def normalise(i):
+            inv_std = stats.tile([P, 1], F32, tag="inv_std")
+            nc.vector.reciprocal(out=inv_std[:], in_=stds[i][:])
+            z = stage.tile([P, D], F32, tag="z", bufs=3)
+            nc.vector.tensor_scalar(
+                out=z[:],
+                in0=r_tiles[i][:],
+                scalar1=neg_means[i][:],
+                scalar2=inv_std[:],
+                op0=ALU.add,
+                op1=ALU.mult,
+            )
+            z_tiles[i] = z
+
+        def turn_normed(i):
+            zt_banks[i] = []
+            for g in range(PASSES):
+                bank = psum_t.tile([P, PACK, P], F32, tag="turned")
+                for t in range(PACK):
+                    u, e = divmod(t, 2)
+                    first = e * BANK + (2 * g + u) * P
+                    nc.tensor.transpose(bank[:, t, :], z_tiles[i][:, first : first + P], ident[:])
+                zt_banks[i].append(bank)
+
+        def affine(i):
+            planes = stage.tile([P, PASSES, PACK, P], BF16, tag="planes")
+            for g in range(PASSES):
+                for t in range(PACK):
+                    j = PACK * g + t
+                    nc.scalar.activation(
+                        out=planes[:, g, t, :],
+                        in_=zt_banks[i][g][:, t, :],
+                        func=ACT.Identity,
+                        scale=gain_shift[:, j : j + 1],
+                        bias=gain_shift[:, ROW_BLOCKS + j : ROW_BLOCKS + j + 1],
+                    )
+            plane_tiles[i] = planes
+
+        def group_normed(i):
+            m_grouped = stage.tile([P, PASSES, P, PACK], BF16, align_bytes=64, tag="m_grouped")
+            nc.vector.tensor_copy(out=m_grouped[:], in_=plane_tiles[i][:].rearrange("p g t r -> p g r t"))
+            m_groupeds[i] = m_grouped
+
+        def quantise_normed(i):
+            quantise(m_groupeds[i][:], m_codes[:, i], m_scales[:, i])
+
+        def feed_forward(i):
+            o_banks[i] = [
+                matmul_group(m_codes[:, i], m_scales[:, i], w2_codes[:, h], w2_scales[:, h])
+                for h in range(HALVES)
+            ]
+
+        def add_bias(i):
+            result = results.tile([P, D], F32, tag="result")
+            for h in range(HALVES):
+                cols = slice(h * BANK, (h + 1) * BANK)
+                nc.vector.tensor_tensor(out=result[:, cols], in0=o_banks[i][h][:], in1=bias_all[:, cols], op=ALU.add)
+            result_tiles[i] = result
+
+        def relu_and_store(i):
+            b, s = divmod(i, SEQS)
+            result = result_tiles[i]
+            nc.vector.tensor_scalar_max(out=result[:], in0=result[:], scalar1=0.0)
+            nc.sync.dma_start(out=out_view[:, b, s, :], in_=result[:])
+
+        both = [nc.scalar.copy, nc.vector.tensor_copy]
+        a_grouped_0 = prepare_tokens(0, both)
+        for e in range(HALVES):
+            w1_grouped = new_w_grouped()
+            for c in range(4):
+                prepare_weight_rows(wout_raw[:, e, c, :], both[c % 2], w1_grouped, c)
+            if e == 0:
+                quantise_tokens(0, a_grouped_0)
+            quantise(w1_grouped[:], w1_codes[:, e], w1_scales[:, e])
+
+        ln_bank = psum_t.tile([P, 4, P], F32, tag="turned")
+        nc.tensor.transpose(ln_bank[:, 0, :], ln_rows[:].bitcast(F32), ident[:])
+        gain_shift = keep.tile([P, 2 * ROW_BLOCKS], F32)
+        nc.vector.tensor_copy(out=gain_shift[:], in_=ln_bank[:, 0, 0:ROW_BLOCKS].bitcast(BF16))
+
+        bias_all = keep.tile([P, D], F32)
+        for h in range(HALVES):
+            cols = slice(h * BANK, (h + 1) * BANK)
+            bias_bank = psum_mm.tile([P, BANK], F32, tag="acc")
+            nc.tensor.matmul(out=bias_bank[:], lhsT=ones[:], rhs=bias_row[:, cols], start=True, stop=True)
+            nc.scalar.copy(out=bias_all[:, cols], in_=bias_bank[:])
+
+        CHUNKS = (TIME_BLOCKS - 1) + ROW_BLOCKS // 2
+        grouped_chunks = {}
+
+        def prepare_chunk(k):
+            if k < TIME_BLOCKS - 1:
+                grouped_chunks[k] = prepare_tokens(k + 1, [nc.scalar.copy, nc.scalar.copy])
+            else:
+                h, first = divmod(2 * (k - (TIME_BLOCKS - 1)), 4)
+                if first == 0:
+                    grouped_chunks[k] = new_w_grouped()
+                else:
+                    grouped_chunks[k] = grouped_chunks[k - 1]
+                for c in (first, first + 1):
+                    prepare_weight_rows(ff1_raw[:, 4 * h + c, :], nc.scalar.copy, grouped_chunks[k], c)
+
+        def quantise_chunk(k):
+            if k < TIME_BLOCKS - 1:
+                quantise_tokens(k + 1, grouped_chunks[k])
+            else:
+                h, first = divmod(2 * (k - (TIME_BLOCKS - 1)), 4)
+                if first == 2:
+                    quantise(grouped_chunks[k][:], w2_codes[:, h], w2_scales[:, h])
+
+        RESIDUAL, NORMALISE, TURN, AFFINE, GROUP, FEED_FORWARD, FINISH = 1, 3, 4, 5, 6, 7, 8
+
+        def live(i):
+            return 0 <= i < TOKEN_BLOCKS
+
+        for n in range(TOKEN_BLOCKS + FINISH):
+            for k in range(CHUNKS):
+                if max(0, k - 1) == n:
+                    prepare_chunk(k)
+            if live(n - NORMALISE):
+                normalise(n - NORMALISE)
+            if live(n - TURN):
+                turn_normed(n - TURN)
+            if live(n - AFFINE):
+                affine(n - AFFINE)
+            if live(n - RESIDUAL):
+                deviation(n - RESIDUAL, add_residual(n - RESIDUAL))
+            for k in range(CHUNKS):
+                if max(0, k - 1) + 1 == n:
+                    quantise_chunk(k)
+            if live(n - FINISH):
+                add_bias(n - FINISH)
+            if live(n - GROUP):
+                group_normed(n - GROUP)
+            if live(n - FINISH):
+                relu_and_store(n - FINISH)
+            if live(n - GROUP):
+                quantise_normed(n - GROUP)
+            if live(n):
+                project(n)
+            if live(n - FEED_FORWARD):
+                feed_forward(n - FEED_FORWARD)

@@ -22,6 +22,7 @@ SEQS = 2
 TIME_BLOCKS = 4
 TOKEN_BLOCKS = SEQS * TIME_BLOCKS
 EPS = 1e-5
+FLOAT32_MAX = 3.4028234663852886e38
 
 FLOPS = 2 * 2 * (SEQS * 512) * D * D
 
@@ -208,7 +209,7 @@ def tile_temporalatt_pb_kernel(tc, ax_cat, features, wout_w, ln_g, ln_b, ff1_w, 
             inv_std = stats.tile([P, 1], F32, tag="inv_std")
             nc.vector.reciprocal(out=inv_std[:], in_=stds[i][:])
             z = stage.tile([P, D], F32, tag="z", bufs=3)
-            nc.vector.tensor_scalar(
+            nc.gpsimd.tensor_scalar(
                 out=z[:],
                 in0=r_tiles[i][:],
                 scalar1=neg_means[i][:],
@@ -266,7 +267,9 @@ def tile_temporalatt_pb_kernel(tc, ax_cat, features, wout_w, ln_g, ln_b, ff1_w, 
         def relu_and_store(i):
             b, s = divmod(i, SEQS)
             result = result_tiles[i]
-            nc.vector.tensor_scalar_max(out=result[:], in0=result[:], scalar1=0.0)
+            nc.gpsimd.tensor_scalar(
+                out=result[:], in0=result[:], scalar1=FLOAT32_MAX, scalar2=0.0, op0=ALU.min, op1=ALU.max
+            )
             nc.sync.dma_start(out=out_view[:, b, s, :], in_=result[:])
 
         both = [nc.scalar.copy, nc.vector.tensor_copy]

@@ -22,7 +22,6 @@ SEQS = 2
 TIME_BLOCKS = 4
 TOKEN_BLOCKS = SEQS * TIME_BLOCKS
 EPS = 1e-5
-FLOAT32_MAX = 3.4028234663852886e38
 
 FLOPS = 2 * 2 * (SEQS * 512) * D * D
 
@@ -163,7 +162,6 @@ def tile_temporalatt_pb_kernel(tc, ax_cat, features, wout_w, ln_g, ln_b, ff1_w, 
         plane_tiles = {}
         m_groupeds = {}
         o_banks = {}
-        result_tiles = {}
 
         def project(i):
             y_banks[i] = [
@@ -257,20 +255,14 @@ def tile_temporalatt_pb_kernel(tc, ax_cat, features, wout_w, ln_g, ln_b, ff1_w, 
                 for h in range(HALVES)
             ]
 
-        def add_bias(i):
+        def finish(i):
+            b, s = divmod(i, SEQS)
             result = results.tile([P, D], F32, tag="result")
             for h in range(HALVES):
                 cols = slice(h * BANK, (h + 1) * BANK)
                 nc.vector.tensor_tensor(out=result[:, cols], in0=o_banks[i][h][:], in1=bias_all[:, cols], op=ALU.add)
-            result_tiles[i] = result
-
-        def relu_and_store(i):
-            b, s = divmod(i, SEQS)
-            result = result_tiles[i]
-            nc.gpsimd.tensor_scalar(
-                out=result[:], in0=result[:], scalar1=FLOAT32_MAX, scalar2=0.0, op0=ALU.min, op1=ALU.max
-            )
-            nc.sync.dma_start(out=out_view[:, b, s, :], in_=result[:])
+                nc.scalar.activation(out=result[:, cols], in_=result[:, cols], func=ACT.Relu)
+                nc.sync.dma_start(out=out_view[:, b, s, cols], in_=result[:, cols])
 
         both = [nc.scalar.copy, nc.vector.tensor_copy]
         a_grouped_0 = prepare_tokens(0, both)
@@ -337,12 +329,10 @@ def tile_temporalatt_pb_kernel(tc, ax_cat, features, wout_w, ln_g, ln_b, ff1_w, 
             for k in range(CHUNKS):
                 if max(0, k - 1) + 1 == n:
                     quantise_chunk(k)
-            if live(n - FINISH):
-                add_bias(n - FINISH)
             if live(n - GROUP):
                 group_normed(n - GROUP)
             if live(n - FINISH):
-                relu_and_store(n - FINISH)
+                finish(n - FINISH)
             if live(n - GROUP):
                 quantise_normed(n - GROUP)
             if live(n):

@@ -243,7 +243,14 @@ def tile_temporalatt_pb_kernel(tc, ax_cat, features, wout_w, ln_g, ln_b, ff1_w, 
 
         def group_normed(i):
             m_grouped = stage.tile([P, PASSES, P, PACK], BF16, align_bytes=64, tag="m_grouped")
-            nc.vector.tensor_copy(out=m_grouped[:], in_=plane_tiles[i][:].rearrange("p g t r -> p g r t"))
+            nc.gpsimd.tensor_scalar(
+                out=m_grouped[:],
+                in0=plane_tiles[i][:].rearrange("p g t r -> p g r t"),
+                scalar1=1.0,
+                scalar2=0.0,
+                op0=ALU.mult,
+                op1=ALU.add,
+            )
             m_groupeds[i] = m_grouped
 
         def quantise_normed(i):
@@ -258,10 +265,11 @@ def tile_temporalatt_pb_kernel(tc, ax_cat, features, wout_w, ln_g, ln_b, ff1_w, 
         def finish(i):
             b, s = divmod(i, SEQS)
             result = results.tile([P, D], F32, tag="result")
-            for h in range(HALVES):
-                cols = slice(h * BANK, (h + 1) * BANK)
+            halves = [slice(h * BANK, (h + 1) * BANK) for h in range(HALVES)]
+            for h, cols in enumerate(halves):
                 nc.vector.tensor_tensor(out=result[:, cols], in0=o_banks[i][h][:], in1=bias_all[:, cols], op=ALU.add)
-                nc.scalar.activation(out=result[:, cols], in_=result[:, cols], func=ACT.Relu)
+            for cols in halves:
+                nc.vector.tensor_scalar_max(out=result[:, cols], in0=result[:, cols], scalar1=0.0)
                 nc.sync.dma_start(out=out_view[:, b, s, cols], in_=result[:, cols])
 
         both = [nc.scalar.copy, nc.vector.tensor_copy]
@@ -315,6 +323,8 @@ def tile_temporalatt_pb_kernel(tc, ax_cat, features, wout_w, ln_g, ln_b, ff1_w, 
             return 0 <= i < TOKEN_BLOCKS
 
         for n in range(TOKEN_BLOCKS + FINISH):
+            if live(n - GROUP):
+                group_normed(n - GROUP)
             for k in range(CHUNKS):
                 if max(0, k - 1) == n:
                     prepare_chunk(k)
@@ -329,8 +339,6 @@ def tile_temporalatt_pb_kernel(tc, ax_cat, features, wout_w, ln_g, ln_b, ff1_w, 
             for k in range(CHUNKS):
                 if max(0, k - 1) + 1 == n:
                     quantise_chunk(k)
-            if live(n - GROUP):
-                group_normed(n - GROUP)
             if live(n - FINISH):
                 finish(n - FINISH)
             if live(n - GROUP):

@@ -55,7 +55,7 @@ def tile_temporalatt_pb_kernel(tc, ax_cat, features, wout_w, ln_g, ln_b, ff1_w, 
         eps_col = keep.tile([P, 1], F32)
         nc.vector.memset(eps_col[:], EPS)
         warm = keep.tile([P, 1], F32)
-        nc.scalar.activation(out=warm[:], in_=eps_col[:], func=ACT.Sqrt)
+        nc.scalar.activation(out=warm[:], in_=eps_col[:], func=ACT.Abs_reciprocal_sqrt)
 
         nc.scalar.dma_start(out=ln_rows[0:4, :], in_=ln_g.rearrange("(c w) -> c w", c=4))
         nc.scalar.dma_start(out=ln_rows[4:8, :], in_=ln_b.rearrange("(c w) -> c w", c=4))
@@ -117,6 +117,14 @@ def tile_temporalatt_pb_kernel(tc, ax_cat, features, wout_w, ln_g, ln_b, ff1_w, 
                 in_=grouped.rearrange("p g r t -> p (g r t)"),
             )
 
+        def quantise_weight_rows(w_grouped, codes, scales, rows):
+            for g in range(PASSES):
+                nc.vector.quantize_mx(
+                    out=codes[:, g, rows].bitcast(FP8X4),
+                    scales=scales[:, g, rows],
+                    in_=w_grouped[:, g, rows, :].rearrange("p r t -> p (r t)"),
+                )
+
         def matmul_group(lhs_codes, lhs_scales, rhs_codes, rhs_scales):
             acc = psum_mm.tile([P, BANK], F32, tag="acc")
             for g in range(PASSES):
@@ -156,7 +164,8 @@ def tile_temporalatt_pb_kernel(tc, ax_cat, features, wout_w, ln_g, ln_b, ff1_w, 
         y_banks = {}
         r_tiles = {}
         neg_means = {}
-        stds = {}
+        sum_sqs = {}
+        inv_stds = {}
         z_tiles = {}
         zt_banks = {}
         plane_tiles = {}
@@ -171,7 +180,7 @@ def tile_temporalatt_pb_kernel(tc, ax_cat, features, wout_w, ln_g, ln_b, ff1_w, 
 
         def add_residual(i):
             b, s = divmod(i, SEQS)
-            r = stage.tile([P, D], F32, tag="r", bufs=4)
+            r = stage.tile([P, D], F32, tag="r", bufs=3)
             sums = stats.tile([P, HALVES], F32, tag="sums")
             x_even_odd = x_raw[:, b, s, :].rearrange("p (q e) -> p e q", e=2)
             for e in range(HALVES):
@@ -187,31 +196,36 @@ def tile_temporalatt_pb_kernel(tc, ax_cat, features, wout_w, ln_g, ln_b, ff1_w, 
             r_tiles[i] = r
             return sums
 
-        def deviation(i, sums):
+        def mean(i, sums):
             scaled = stats.tile([P, HALVES], F32, tag="scaled")
             neg_mean = stats.tile([P, 1], F32, tag="neg_mean")
             nc.scalar.activation(
                 out=scaled[:], in_=sums[:], func=ACT.Identity, scale=-1.0 / D, accum_out=neg_mean[:]
             )
+            neg_means[i] = neg_mean
+
+        def squared_deviations(i):
             squares = stage.tile([P, D], BF16, tag="squares")
             sum_sq = stats.tile([P, 1], F32, tag="sum_sq")
             nc.scalar.activation(
-                out=squares[:], in_=r_tiles[i][:], func=ACT.Square, bias=neg_mean[:], accum_out=sum_sq[:]
+                out=squares[:], in_=r_tiles[i][:], func=ACT.Square, bias=neg_means[i][:], accum_out=sum_sq[:]
             )
-            std = stats.tile([P, 1], F32, tag="std")
-            nc.scalar.activation(out=std[:], in_=sum_sq[:], func=ACT.Sqrt, scale=1.0 / D, bias=eps_col[:])
-            neg_means[i] = neg_mean
-            stds[i] = std
+            sum_sqs[i] = sum_sq
+
+        def inverse_deviation(i):
+            inv_std = stats.tile([P, 1], F32, tag="inv_std")
+            nc.scalar.activation(
+                out=inv_std[:], in_=sum_sqs[i][:], func=ACT.Abs_reciprocal_sqrt, scale=1.0 / D, bias=eps_col[:]
+            )
+            inv_stds[i] = inv_std
 
         def normalise(i):
-            inv_std = stats.tile([P, 1], F32, tag="inv_std")
-            nc.vector.reciprocal(out=inv_std[:], in_=stds[i][:])
             z = stage.tile([P, D], F32, tag="z", bufs=3)
             nc.gpsimd.tensor_scalar(
                 out=z[:],
                 in0=r_tiles[i][:],
                 scalar1=neg_means[i][:],
-                scalar2=inv_std[:],
+                scalar2=inv_stds[i][:],
                 op0=ALU.add,
                 op1=ALU.mult,
             )
@@ -227,19 +241,18 @@ def tile_temporalatt_pb_kernel(tc, ax_cat, features, wout_w, ln_g, ln_b, ff1_w, 
                     nc.tensor.transpose(bank[:, t, :], z_tiles[i][:, first : first + P], ident[:])
                 zt_banks[i].append(bank)
 
-        def affine(i):
-            planes = stage.tile([P, PASSES, PACK, P], BF16, tag="planes")
-            for g in range(PASSES):
-                for t in range(PACK):
-                    j = PACK * g + t
-                    nc.scalar.activation(
-                        out=planes[:, g, t, :],
-                        in_=zt_banks[i][g][:, t, :],
-                        func=ACT.Identity,
-                        scale=gain_shift[:, j : j + 1],
-                        bias=gain_shift[:, ROW_BLOCKS + j : ROW_BLOCKS + j + 1],
-                    )
-            plane_tiles[i] = planes
+        def affine(i, g):
+            if g == 0:
+                plane_tiles[i] = stage.tile([P, PASSES, PACK, P], BF16, tag="planes", name="planes")
+            for t in range(PACK):
+                j = PACK * g + t
+                nc.scalar.activation(
+                    out=plane_tiles[i][:, g, t, :],
+                    in_=zt_banks[i][g][:, t, :],
+                    func=ACT.Identity,
+                    scale=gain_shift[:, j : j + 1],
+                    bias=gain_shift[:, ROW_BLOCKS + j : ROW_BLOCKS + j + 1],
+                )
 
         def group_normed(i):
             m_grouped = stage.tile([P, PASSES, P, PACK], BF16, align_bytes=64, tag="m_grouped")
@@ -274,13 +287,21 @@ def tile_temporalatt_pb_kernel(tc, ax_cat, features, wout_w, ln_g, ln_b, ff1_w, 
 
         both = [nc.scalar.copy, nc.vector.tensor_copy]
         a_grouped_0 = prepare_tokens(0, both)
-        for e in range(HALVES):
-            w1_grouped = new_w_grouped()
-            for c in range(4):
-                prepare_weight_rows(wout_raw[:, e, c, :], both[c % 2], w1_grouped, c)
-            if e == 0:
+        w1_grouped = [new_w_grouped() for e in range(HALVES)]
+
+        def quantise_wout_chunk(e, first):
+            rows = slice(first * P, (first + 2) * P)
+            quantise_weight_rows(w1_grouped[e], w1_codes[:, e], w1_scales[:, e], rows)
+
+        wout_chunks = [(e, first) for e in range(HALVES) for first in (0, 2)]
+        for k, (e, first) in enumerate(wout_chunks):
+            for c in (first, first + 1):
+                prepare_weight_rows(wout_raw[:, e, c, :], both[c % 2], w1_grouped[e], c)
+            if k == 0:
                 quantise_tokens(0, a_grouped_0)
-            quantise(w1_grouped[:], w1_codes[:, e], w1_scales[:, e])
+            else:
+                quantise_wout_chunk(*wout_chunks[k - 1])
+        quantise_wout_chunk(*wout_chunks[-1])
 
         ln_bank = psum_t.tile([P, 4, P], F32, tag="turned")
         nc.tensor.transpose(ln_bank[:, 0, :], ln_rows[:].bitcast(F32), ident[:])
@@ -294,30 +315,28 @@ def tile_temporalatt_pb_kernel(tc, ax_cat, features, wout_w, ln_g, ln_b, ff1_w, 
             nc.tensor.matmul(out=bias_bank[:], lhsT=ones[:], rhs=bias_row[:, cols], start=True, stop=True)
             nc.scalar.copy(out=bias_all[:, cols], in_=bias_bank[:])
 
-        CHUNKS = (TIME_BLOCKS - 1) + ROW_BLOCKS // 2
+        TOKEN_CHUNKS = TIME_BLOCKS - 1
+        CHUNKS = TOKEN_CHUNKS + ROW_BLOCKS // 2
         grouped_chunks = {}
 
         def prepare_chunk(k):
-            if k < TIME_BLOCKS - 1:
+            if k < TOKEN_CHUNKS:
                 grouped_chunks[k] = prepare_tokens(k + 1, [nc.scalar.copy, nc.scalar.copy])
             else:
-                h, first = divmod(2 * (k - (TIME_BLOCKS - 1)), 4)
-                if first == 0:
-                    grouped_chunks[k] = new_w_grouped()
-                else:
-                    grouped_chunks[k] = grouped_chunks[k - 1]
+                h, first = divmod(2 * (k - TOKEN_CHUNKS), 4)
+                grouped_chunks[k] = new_w_grouped() if first == 0 else grouped_chunks[k - 1]
                 for c in (first, first + 1):
                     prepare_weight_rows(ff1_raw[:, 4 * h + c, :], nc.scalar.copy, grouped_chunks[k], c)
 
         def quantise_chunk(k):
-            if k < TIME_BLOCKS - 1:
+            if k < TOKEN_CHUNKS:
                 quantise_tokens(k + 1, grouped_chunks[k])
             else:
-                h, first = divmod(2 * (k - (TIME_BLOCKS - 1)), 4)
-                if first == 2:
-                    quantise(grouped_chunks[k][:], w2_codes[:, h], w2_scales[:, h])
+                h, first = divmod(2 * (k - TOKEN_CHUNKS), 4)
+                rows = slice(first * P, (first + 2) * P)
+                quantise_weight_rows(grouped_chunks[k], w2_codes[:, h], w2_scales[:, h], rows)
 
-        RESIDUAL, NORMALISE, TURN, AFFINE, GROUP, FEED_FORWARD, FINISH = 1, 3, 4, 5, 6, 7, 8
+        RESIDUAL, NORMALISE, TURN, AFFINE, GROUP, FEED_FORWARD, FINISH = 1, 2, 3, 4, 5, 6, 7
 
         def live(i):
             return 0 <= i < TOKEN_BLOCKS
@@ -325,17 +344,25 @@ def tile_temporalatt_pb_kernel(tc, ax_cat, features, wout_w, ln_g, ln_b, ff1_w, 
         for n in range(TOKEN_BLOCKS + FINISH):
             if live(n - GROUP):
                 group_normed(n - GROUP)
-            for k in range(CHUNKS):
-                if max(0, k - 1) == n:
-                    prepare_chunk(k)
             if live(n - NORMALISE):
                 normalise(n - NORMALISE)
             if live(n - TURN):
                 turn_normed(n - TURN)
-            if live(n - AFFINE):
-                affine(n - AFFINE)
             if live(n - RESIDUAL):
-                deviation(n - RESIDUAL, add_residual(n - RESIDUAL))
+                sums = add_residual(n - RESIDUAL)
+            if live(n - AFFINE):
+                affine(n - AFFINE, 0)
+            if live(n - RESIDUAL):
+                mean(n - RESIDUAL, sums)
+            if live(n - AFFINE):
+                affine(n - AFFINE, 1)
+            if live(n - RESIDUAL):
+                squared_deviations(n - RESIDUAL)
+            for k in range(CHUNKS):
+                if max(0, k - 1) == n:
+                    prepare_chunk(k)
+            if live(n - RESIDUAL):
+                inverse_deviation(n - RESIDUAL)
             for k in range(CHUNKS):
                 if max(0, k - 1) + 1 == n:
                     quantise_chunk(k)

from contextlib import ExitStack

import concourse.mybir as mybir
from concourse.masks import make_identity

F32 = mybir.dt.float32
BF16 = mybir.dt.bfloat16
U32 = mybir.dt.uint32
U8 = mybir.dt.uint8
FP8X4 = mybir.dt.float8_e4m3fn_x4
ACT = mybir.ActivationFunctionType
ALU = mybir.AluOpType

P = 128
PACK = 4
D = 1024
PASSES = D // (P * PACK)
BANK = 512
HALVES = D // BANK
ROW_BLOCKS = D // P
SEQS = 2
TIME_BLOCKS = 4
TOKEN_BLOCKS = SEQS * TIME_BLOCKS
EPS = 1e-5

FLOPS = 2 * 2 * (SEQS * 512) * D * D


def tile_temporalatt_pb_kernel(tc, ax_cat, features, wout_w, ln_g, ln_b, ff1_w, ff1_b, out):
    nc = tc.nc

    ax_view = ax_cat.rearrange("s (b p) k -> p b s k", p=P)
    x_view = features.rearrange("o (b p) s d -> p (o b) s d", p=P)
    out_view = out.rearrange("s (b p) f -> p b s f", p=P)
    wout_view = wout_w.rearrange("(c p e) k -> p e c k", p=P, e=2)
    ff1_view = ff1_w.rearrange("(j p) k -> p j k", p=P)

    with ExitStack() as stack:
        stack.enter_context(tc.manual_schedule())
        keep = stack.enter_context(tc.tile_pool(name="keep", bufs=1))
        stage = stack.enter_context(tc.tile_pool(name="stage", bufs=2))
        stats = stack.enter_context(tc.tile_pool(name="stats", bufs=4))
        results = stack.enter_context(tc.tile_pool(name="results", bufs=3))
        psum_t = stack.enter_context(tc.psum_pool(name="psum_t", bufs=4))
        psum_mm = stack.enter_context(tc.psum_pool(name="psum_mm", bufs=4))

        ident = keep.tile([P, P], F32)
        make_identity(nc, ident[:])
        ones = keep.tile([P, P], BF16)
        nc.gpsimd.memset(ones[:], 1.0)
        bias_row = keep.tile([P, D], BF16)
        nc.gpsimd.memset(bias_row[:], 0.0)
        ln_rows = keep.tile([P, 2 * P], BF16)
        nc.gpsimd.memset(ln_rows[:], 0.0)
        eps_col = keep.tile([P, 1], F32)
        nc.vector.memset(eps_col[:], EPS)
        warm = keep.tile([P, 1], F32)
        nc.scalar.activation(out=warm[:], in_=eps_col[:], func=ACT.Abs_reciprocal_sqrt)

        nc.scalar.dma_start(out=ln_rows[0:4, :], in_=ln_g.rearrange("(c w) -> c w", c=4))
        nc.scalar.dma_start(out=ln_rows[4:8, :], in_=ln_b.rearrange("(c w) -> c w", c=4))
        nc.scalar.dma_start(out=bias_row[0:1, :], in_=ff1_b.rearrange("(o f) -> o f", o=1))

        wout_raw = keep.tile([P, 2, 4, D], BF16)
        ax_raw = keep.tile([P, TIME_BLOCKS, SEQS, D], BF16)
        x_raw = keep.tile([P, TIME_BLOCKS, SEQS, D], BF16)
        ff1_raw = keep.tile([P, ROW_BLOCKS, D], BF16)

        def load_ax(b):
            nc.sync.dma_start(out=ax_raw[:, b], in_=ax_view[:, b])

        def load_x(b):
            nc.sync.dma_start(out=x_raw[:, b], in_=x_view[:, b])

        def load_ff1(j):
            nc.sync.dma_start(out=ff1_raw[:, j : j + 2], in_=ff1_view[:, j : j + 2])

        load_ax(0)
        for e in range(2):
            for c in range(0, 4, 2):
                nc.sync.dma_start(out=wout_raw[:, e, c : c + 2], in_=wout_view[:, e, c : c + 2])
        load_x(0)
        load_ax(1)
        load_ax(2)
        load_x(1)
        load_ax(3)
        load_ff1(0)
        load_ff1(2)
        load_x(2)
        load_ff1(4)
        load_ff1(6)
        load_x(3)

        w1_codes = keep.tile([P, HALVES, PASSES, BANK], U32, align_bytes=64)
        w1_scales = keep.tile([P, HALVES, PASSES, BANK], U8, align_bytes=64)
        w2_codes = keep.tile([P, HALVES, PASSES, BANK], U32, align_bytes=64)
        w2_scales = keep.tile([P, HALVES, PASSES, BANK], U8, align_bytes=64)
        a_codes = keep.tile([P, TOKEN_BLOCKS, PASSES, P], U32, align_bytes=64)
        a_scales = keep.tile([P, TOKEN_BLOCKS, PASSES, P], U8, align_bytes=64)
        m_codes = keep.tile([P, TOKEN_BLOCKS, PASSES, P], U32, align_bytes=64)
        m_scales = keep.tile([P, TOKEN_BLOCKS, PASSES, P], U8, align_bytes=64)

        def turn_rows(raw_rows):
            words = raw_rows.bitcast(F32)
            bank = psum_t.tile([P, 4, P], F32, tag="turned")
            for c in range(4):
                nc.tensor.transpose(bank[:, c, :], words[:, c * P : (c + 1) * P], ident[:])
            return bank

        def group_rows(copy, bank, grouped_rows):
            copy(out=grouped_rows.bitcast(F32), in_=bank[:].rearrange("p (g u) r -> p g r u", u=2))

        def quantise(grouped, codes, scales):
            nc.vector.quantize_mx(
                out=codes.rearrange("p g r -> p (g r)").bitcast(FP8X4),
                scales=scales.rearrange("p g r -> p (g r)"),
                in_=grouped.rearrange("p g r t -> p (g r t)"),
            )

        def quantise_weight_rows(w_grouped, codes, scales, rows):
            for g in range(PASSES):
                nc.vector.quantize_mx(
                    out=codes[:, g, rows].bitcast(FP8X4),
                    scales=scales[:, g, rows],
                    in_=w_grouped[:, g, rows, :].rearrange("p r t -> p (r t)"),
                )

        def matmul_group(lhs_codes, lhs_scales, rhs_codes, rhs_scales):
            acc = psum_mm.tile([P, BANK], F32, tag="acc")
            for g in range(PASSES):
                nc.tensor.matmul_mx(
                    out=acc[:],
                    lhsT=lhs_codes[:, g, :].bitcast(FP8X4),
                    lhsT_scale=lhs_scales[:, g, :],
                    rhs=rhs_codes[:, g, :].bitcast(FP8X4),
                    rhs_scale=rhs_scales[:, g, :],
                    start=(g == 0),
                    stop=(g == PASSES - 1),
                )
            return acc

        def prepare_tokens(b, copies):
            a_grouped = stage.tile([P, SEQS * PASSES, P, PACK], BF16, align_bytes=64, tag="a_grouped", bufs=3)
            for s in range(SEQS):
                bank = turn_rows(ax_raw[:, b, s, :])
                group_rows(copies[s], bank, a_grouped[:, s * PASSES : (s + 1) * PASSES])
            return a_grouped

        def quantise_tokens(b, a_grouped):
            first = SEQS * b
            nc.vector.quantize_mx(
                out=a_codes[:, first : first + SEQS].rearrange("p i g r -> p (i g r)").bitcast(FP8X4),
                scales=a_scales[:, first : first + SEQS].rearrange("p i g r -> p (i g r)"),
                in_=a_grouped[:].rearrange("p g r t -> p (g r t)"),
            )

        def prepare_weight_rows(raw_rows, copy, w_grouped, c):
            group_rows(copy, turn_rows(raw_rows), w_grouped[:, :, c * P : (c + 1) * P, :])

        def new_w_grouped():
            w_grouped = stage.tile([P, PASSES, BANK, PACK], BF16, align_bytes=64, tag="w_grouped")
            return w_grouped

        y_banks = {}
        r_tiles = {}
        neg_means = {}
        sum_sqs = {}
        inv_stds = {}
        z_tiles = {}
        zt_banks = {}
        plane_tiles = {}
        m_groupeds = {}
        o_banks = {}

        def project(i):
            y_banks[i] = [
                matmul_group(a_codes[:, i], a_scales[:, i], w1_codes[:, e], w1_scales[:, e])
                for e in range(HALVES)
            ]

        def add_residual(i):
            b, s = divmod(i, SEQS)
            r = stage.tile([P, D], F32, tag="r", bufs=3)
            sums = stats.tile([P, HALVES], F32, tag="sums")
            x_even_odd = x_raw[:, b, s, :].rearrange("p (q e) -> p e q", e=2)
            for e in range(HALVES):
                nc.vector.scalar_tensor_tensor(
                    out=r[:, e * BANK : (e + 1) * BANK],
                    in0=y_banks[i][e][:],
                    scalar=1.0,
                    in1=x_even_odd[:, e, :],
                    op0=ALU.mult,
                    op1=ALU.add,
                    accum_out=sums[:, e : e + 1],
                )
            r_tiles[i] = r
            return sums

        def mean(i, sums):
            scaled = stats.tile([P, HALVES], F32, tag="scaled")
            neg_mean = stats.tile([P, 1], F32, tag="neg_mean")
            nc.scalar.activation(
                out=scaled[:], in_=sums[:], func=ACT.Identity, scale=-1.0 / D, accum_out=neg_mean[:]
            )
            neg_means[i] = neg_mean

        def squared_deviations(i):
            squares = stage.tile([P, D], BF16, tag="squares")
            sum_sq = stats.tile([P, 1], F32, tag="sum_sq")
            nc.scalar.activation(
                out=squares[:], in_=r_tiles[i][:], func=ACT.Square, bias=neg_means[i][:], accum_out=sum_sq[:]
            )
            sum_sqs[i] = sum_sq

        def inverse_deviation(i):
            inv_std = stats.tile([P, 1], F32, tag="inv_std")
            nc.scalar.activation(
                out=inv_std[:], in_=sum_sqs[i][:], func=ACT.Abs_reciprocal_sqrt, scale=1.0 / D, bias=eps_col[:]
            )
            inv_stds[i] = inv_std

        def normalise(i):
            z = stage.tile([P, D], F32, tag="z", bufs=3)
            nc.gpsimd.tensor_scalar(
                out=z[:],
                in0=r_tiles[i][:],
                scalar1=neg_means[i][:],
                scalar2=inv_stds[i][:],
                op0=ALU.add,
                op1=ALU.mult,
            )
            z_tiles[i] = z

        def turn_normed(i):
            zt_banks[i] = []
            for g in range(PASSES):
                bank = psum_t.tile([P, PACK, P], F32, tag="turned")
                for t in range(PACK):
                    u, e = divmod(t, 2)
                    first = e * BANK + (2 * g + u) * P
                    nc.tensor.transpose(bank[:, t, :], z_tiles[i][:, first : first + P], ident[:])
                zt_banks[i].append(bank)

        def affine(i, g):
            if g == 0:
                plane_tiles[i] = stage.tile([P, PASSES, PACK, P], BF16, tag="planes", name="planes")
            for t in range(PACK):
                j = PACK * g + t
                nc.scalar.activation(
                    out=plane_tiles[i][:, g, t, :],
                    in_=zt_banks[i][g][:, t, :],
                    func=ACT.Identity,
                    scale=gain_shift[:, j : j + 1],
                    bias=gain_shift[:, ROW_BLOCKS + j : ROW_BLOCKS + j + 1],
                )

        def group_normed(i):
            m_grouped = stage.tile([P, PASSES, P, PACK], BF16, align_bytes=64, tag="m_grouped")
            nc.gpsimd.tensor_scalar(
                out=m_grouped[:],
                in0=plane_tiles[i][:].rearrange("p g t r -> p g r t"),
                scalar1=1.0,
                scalar2=0.0,
                op0=ALU.mult,
                op1=ALU.add,
            )
            m_groupeds[i] = m_grouped

        def quantise_normed(i):
            quantise(m_groupeds[i][:], m_codes[:, i], m_scales[:, i])

        def feed_forward(i):
            o_banks[i] = [
                matmul_group(m_codes[:, i], m_scales[:, i], w2_codes[:, h], w2_scales[:, h])
                for h in range(HALVES)
            ]

        def finish(i):
            b, s = divmod(i, SEQS)
            result = results.tile([P, D], F32, tag="result")
            halves = [slice(h * BANK, (h + 1) * BANK) for h in range(HALVES)]
            for h, cols in enumerate(halves):
                nc.vector.tensor_tensor(out=result[:, cols], in0=o_banks[i][h][:], in1=bias_all[:, cols], op=ALU.add)
            for cols in halves:
                nc.vector.tensor_scalar_max(out=result[:, cols], in0=result[:, cols], scalar1=0.0)
                nc.sync.dma_start(out=out_view[:, b, s, cols], in_=result[:, cols])

        both = [nc.scalar.copy, nc.vector.tensor_copy]
        a_grouped_0 = prepare_tokens(0, both)
        w1_grouped = [new_w_grouped() for e in range(HALVES)]

        def quantise_wout_chunk(e, first):
            rows = slice(first * P, (first + 2) * P)
            quantise_weight_rows(w1_grouped[e], w1_codes[:, e], w1_scales[:, e], rows)

        wout_chunks = [(e, first) for e in range(HALVES) for first in (0, 2)]
        for k, (e, first) in enumerate(wout_chunks):
            for c in (first, first + 1):
                prepare_weight_rows(wout_raw[:, e, c, :], both[c % 2], w1_grouped[e], c)
            if k == 0:
                quantise_tokens(0, a_grouped_0)
            else:
                quantise_wout_chunk(*wout_chunks[k - 1])
        quantise_wout_chunk(*wout_chunks[-1])

        ln_bank = psum_t.tile([P, 4, P], F32, tag="turned")
        nc.tensor.transpose(ln_bank[:, 0, :], ln_rows[:].bitcast(F32), ident[:])
        gain_shift = keep.tile([P, 2 * ROW_BLOCKS], F32)
        nc.vector.tensor_copy(out=gain_shift[:], in_=ln_bank[:, 0, 0:ROW_BLOCKS].bitcast(BF16))

        bias_all = keep.tile([P, D], F32)
        for h in range(HALVES):
            cols = slice(h * BANK, (h + 1) * BANK)
            bias_bank = psum_mm.tile([P, BANK], F32, tag="acc")
            nc.tensor.matmul(out=bias_bank[:], lhsT=ones[:], rhs=bias_row[:, cols], start=True, stop=True)
            nc.scalar.copy(out=bias_all[:, cols], in_=bias_bank[:])

        TOKEN_CHUNKS = TIME_BLOCKS - 1
        CHUNKS = TOKEN_CHUNKS + ROW_BLOCKS // 2
        grouped_chunks = {}

        def prepare_chunk(k):
            if k < TOKEN_CHUNKS:
                grouped_chunks[k] = prepare_tokens(k + 1, [nc.scalar.copy, nc.scalar.copy])
            else:
                h, first = divmod(2 * (k - TOKEN_CHUNKS), 4)
                grouped_chunks[k] = new_w_grouped() if first == 0 else grouped_chunks[k - 1]
                for c in (first, first + 1):
                    prepare_weight_rows(ff1_raw[:, 4 * h + c, :], nc.scalar.copy, grouped_chunks[k], c)

        def quantise_chunk(k):
            if k < TOKEN_CHUNKS:
                quantise_tokens(k + 1, grouped_chunks[k])
            else:
                h, first = divmod(2 * (k - TOKEN_CHUNKS), 4)
                rows = slice(first * P, (first + 2) * P)
                quantise_weight_rows(grouped_chunks[k], w2_codes[:, h], w2_scales[:, h], rows)

        RESIDUAL, NORMALISE, TURN, AFFINE, GROUP, FEED_FORWARD, FINISH = 1, 2, 3, 4, 5, 6, 7

        def live(i):
            return 0 <= i < TOKEN_BLOCKS

        for n in range(TOKEN_BLOCKS + FINISH):
            if live(n - GROUP):
                group_normed(n - GROUP)
            if live(n - NORMALISE):
                normalise(n - NORMALISE)
            if live(n - TURN):
                turn_normed(n - TURN)
            if live(n - RESIDUAL):
                sums = add_residual(n - RESIDUAL)
            if live(n - AFFINE):
                affine(n - AFFINE, 0)
            if live(n - RESIDUAL):
                mean(n - RESIDUAL, sums)
            if live(n - AFFINE):
                affine(n - AFFINE, 1)
            if live(n - RESIDUAL):
                squared_deviations(n - RESIDUAL)
            for k in range(CHUNKS):
                if max(0, k - 1) == n:
                    prepare_chunk(k)
            if live(n - RESIDUAL):
                inverse_deviation(n - RESIDUAL)
            for k in range(CHUNKS):
                if max(0, k - 1) + 1 == n:
                    quantise_chunk(k)
            if live(n - FINISH):
                finish(n - FINISH)
            if live(n - GROUP):
                quantise_normed(n - GROUP)
            if live(n):
                project(n)
            if live(n - FEED_FORWARD):
                feed_forward(n - FEED_FORWARD)
